import numpy as np
import ml_dtypes


def mxq(x, axis, fmt="e4m3"):
    dtype, down = {"e4m3": (ml_dtypes.float8_e4m3fn, 7), "e5m2": (ml_dtypes.float8_e5m2, 14)}[fmt]
    v = np.moveaxis(np.asarray(x, np.float32).astype(ml_dtypes.bfloat16).astype(np.float64), axis, -1)
    blocks = v.reshape(v.shape[:-1] + (-1, 32))
    amax = np.abs(blocks).max(-1, keepdims=True)
    byte = np.maximum(np.where(amax > 0, np.frexp(amax)[1] - 1 + 127, 0) - down, 1)
    scale = np.exp2(byte - 127.0)
    codes = (blocks / scale).astype(np.float32).astype(dtype).astype(np.float64)
    return np.moveaxis((codes * scale).reshape(v.shape), -1, axis)


WIDE = False


def mx_kscale(k):
    if not WIDE:
        return np.ones(k)
    levels = np.array([10, -10, 5, -5, 0])
    a = np.random.permutation(np.resize(levels, k // 512 * 4)).reshape(k // 512, 4)
    idx = np.arange(k)
    return np.exp2(a[idx // 512, idx % 128 // 32])


BF16 = ml_dtypes.bfloat16


def bf(x):
    return np.asarray(x, np.float32).astype(BF16)


def f64(x):
    return np.asarray(x).astype(np.float64)


B, N, D_IN, H, D_HEAD, D_EXPAND = 8, 1024, 512, 1, 64, 2048
D_Q = D_HEAD * H
D_V = D_IN * H
D_QKV = 2 * D_Q + D_V
EPS = 1e-5


def feature_norm(x, gamma, beta):
    mean = x.mean(axis=1, keepdims=True)
    var = x.var(axis=1, keepdims=True)
    return gamma * (x - mean) / np.sqrt(var + EPS) + beta


def sigmoid(v):
    e = np.exp(-np.abs(v))
    return np.where(v >= 0.0, 1.0, e) / (1.0 + e)


def swish(v):
    return v * sigmoid(v)


def setup_inputs():
    wcol = np.concatenate([np.full(2 * D_Q, 1.9 / np.sqrt(D_HEAD * D_IN)), np.full(D_V, 0.5 / np.sqrt(D_IN))])
    bcol = np.concatenate([np.full(2 * D_Q, 0.03), np.full(D_V, 0.1)])
    s = mx_kscale(D_IN)
    t = s / s.min()
    return {"x": bf(1.5 * np.random.standard_normal((B, N, D_IN)) + 0.5 * np.random.standard_normal((1, 1, D_IN))),
            "pos_enc": bf(np.random.standard_normal((1, N, D_IN)) * t),
            "gamma1": bf((1.0 + 0.1 * np.random.standard_normal((1, 1, D_IN))) * t),
            "beta1": bf(0.1 * np.random.standard_normal((1, 1, D_IN)) * t),
            "W_qkv": bf(np.random.standard_normal((D_IN, D_QKV)) * wcol / t[:, None]),
            "b_qkv": bf(np.random.standard_normal(D_QKV) * bcol)}


def reference(x, pos_enc, gamma1, beta1, W_qkv, b_qkv):
    h = feature_norm(f64(x), f64(gamma1), f64(beta1)) + f64(pos_enc)
    a = swish(h)
    return (mxq(a, 2, "e4m3") @ mxq(f64(W_qkv), 0, "e4m3")) + f64(b_qkv)

@@ -1,0 +1,290 @@
+from contextlib import ExitStack
+
+import concourse.masks as masks
+import concourse.mybir as mybir
+
+F32 = mybir.dt.float32
+BF16 = mybir.dt.bfloat16
+U32 = mybir.dt.uint32
+U8 = mybir.dt.uint8
+FP8X4 = mybir.dt.float8_e4m3fn_x4
+ACT = mybir.ActivationFunctionType
+ALU = mybir.AluOpType
+
+P = 128
+PACK = 4
+BATCH = 8
+TOKENS = 1024
+D_IN = P * PACK
+D_OUT = 640
+TILES = TOKENS // P
+HALF_TILES = TILES // 2
+HALF = TOKENS // 2
+PAIR = PACK // 2
+WIDE = 512
+NARROW = D_OUT - WIDE
+BANKS_PER_HALF = 1 + HALF_TILES
+FILLS = 2 * BANKS_PER_HALF
+AHEAD = 3
+STORE_TILES = 2
+EPS = 1e-5
+
+FLOPS = 2 * BATCH * TOKENS * D_IN * D_OUT
+
+
+def tile_attentionblock_pa_t_kernel(tc, x, pos_enc, gamma1, beta1, W_qkv, b_qkv, out):
+    nc = tc.nc
+    with ExitStack() as ctx:
+        const = ctx.enter_context(tc.tile_pool(name="const", bufs=1))
+        work = ctx.enter_context(tc.tile_pool(name="work", bufs=2))
+        small = ctx.enter_context(tc.tile_pool(name="small", bufs=4))
+        psum = ctx.enter_context(tc.psum_pool(name="psum", bufs=1))
+        ctx.enter_context(tc.manual_schedule())
+
+        gb_rows = const.tile([P, P], BF16)
+        nc.vector.memset(gb_rows[:], 0.0)
+
+        x_nat = {}
+
+        def load_x(b):
+            x_nat[b] = const.tile([P, TILES, D_IN], BF16, name="x%d" % b)
+            nc.sync.dma_start(out=x_nat[b][:], in_=x[b, :, :].rearrange("(p j) d -> p j d", j=TILES))
+
+        load_x(0)
+        nc.sync.dma_start(out=gb_rows[0:PACK, :], in_=gamma1[0, :, :].rearrange("a (t p) -> (a t) p", p=P))
+        nc.sync.dma_start(out=gb_rows[PACK : 2 * PACK, :], in_=beta1[0, :, :].rearrange("a (t p) -> (a t) p", p=P))
+        pos_nat = const.tile([P, TILES, D_IN], BF16)
+        nc.sync.dma_start(out=pos_nat[:], in_=pos_enc[0, :, :].rearrange("(p j) d -> p j d", j=TILES))
+        load_x(1)
+        w_raw = const.tile([P, PACK, D_OUT], BF16)
+        nc.sync.dma_start(out=w_raw[:], in_=W_qkv.rearrange("(t p) n -> p t n", p=P))
+        bias_bc = const.tile([P, D_OUT], BF16)
+        nc.sync.dma_start(out=bias_bc[:], in_=b_qkv.partition_broadcast(P))
+        for b in range(2, BATCH):
+            load_x(b)
+
+        ident = const.tile([P, P], BF16)
+        masks.make_identity(nc, ident[:])
+        ones = const.tile([P, 1], BF16)
+        nc.vector.memset(ones[:], 1.0)
+        minus_half = const.tile([P, PAIR], F32)
+        nc.vector.memset(minus_half[:], -0.5)
+        warm = const.tile([P, 1], F32)
+        nc.vector.memset(warm[:], 0.0)
+        nc.scalar.activation(out=warm[:], in_=warm[:], func=ACT.Silu)
+
+        neg_mean, sum_sq, var_eps, scale, shift = {}, {}, {}, {}, {}
+        x_t, h_pl, a_pl, a_grp, a_codes, a_scales = {}, {}, {}, {}, {}, {}
+        prod, out_sb = {}, {}
+
+        def token_sums(b):
+            sums = psum.tile([P, PACK], F32, name="sums")
+            for t in range(PACK):
+                for j in range(TILES):
+                    nc.tensor.matmul(
+                        out=sums[:, t : t + 1],
+                        lhsT=x_nat[b][:, j, t * P : (t + 1) * P],
+                        rhs=ones[:],
+                        start=(j == 0),
+                        stop=(j == TILES - 1),
+                    )
+            neg_mean[b] = small.tile([P, PACK], F32, name="neg_mean")
+            nc.scalar.activation(out=neg_mean[b][:], in_=sums[:], func=ACT.Copy, scale=-1.0 / TOKENS)
+            sum_sq[b] = small.tile([P, PACK], F32, name="sum_sq")
+            var_eps[b] = small.tile([P, PACK], F32, name="var_eps")
+            scale[b] = small.tile([P, PACK], F32, name="scale")
+            shift[b] = small.tile([P, PACK], F32, name="shift")
+
+        def transpose_plane(b, t):
+            x_t[b, t] = psum.tile([P, TOKENS], BF16, name="x_t", tag="x_t%d" % t)
+            for j in range(TILES):
+                nc.tensor.transpose(x_t[b, t][:, j * P : (j + 1) * P], x_nat[b][:, j, t * P : (t + 1) * P], ident[:])
+
+        def centred_squares(b, t):
+            unused = work.tile([P, TOKENS], BF16, name="unused")
+            nc.scalar.activation(
+                out=unused[:],
+                in_=x_t[b, t][:],
+                func=ACT.Square,
+                bias=neg_mean[b][:, t : t + 1],
+                scale=1.0,
+                accum_out=sum_sq[b][:, t : t + 1],
+            )
+
+        def scale_of(b, pair):
+            planes = slice(pair * PAIR, (pair + 1) * PAIR)
+            nc.scalar.activation(
+                out=var_eps[b][:, planes], in_=sum_sq[b][:, planes], func=ACT.Copy, scale=1.0 / TOKENS, bias=EPS
+            )
+            rstd = small.tile([P, PAIR], F32, name="rstd")
+            nc.gpsimd.tensor_tensor(out=rstd[:], in0=var_eps[b][:, planes], in1=minus_half[:], op=ALU.pow)
+            nc.gpsimd.tensor_tensor(out=scale[b][:, planes], in0=rstd[:], in1=gamma[:, planes], op=ALU.mult)
+
+        def shift_of(b):
+            for t in range(PACK):
+                nc.scalar.activation(
+                    out=shift[b][:, t : t + 1],
+                    in_=neg_mean[b][:, t : t + 1],
+                    func=ACT.Identity,
+                    scale=scale[b][:, t : t + 1],
+                    bias=beta[:, t : t + 1],
+                )
+
+        def normalise_plane(b, t):
+            if t == 0:
+                h_pl[b] = work.tile([P, PACK, TOKENS], F32, name="h_pl")
+            nc.vector.scalar_tensor_tensor(
+                out=h_pl[b][:, t, :],
+                in0=x_t[b, t][:],
+                scalar=scale[b][:, t : t + 1],
+                in1=pos_t[:, t, :],
+                op0=ALU.mult,
+                op1=ALU.add,
+            )
+
+        def swish(b, half):
+            if half == 0:
+                a_pl[b] = work.tile([P, PACK, TOKENS], BF16, name="a_pl")
+            cols = slice(half * HALF, (half + 1) * HALF)
+            for t in range(PACK):
+                nc.scalar.activation(
+                    out=a_pl[b][:, t, cols], in_=h_pl[b][:, t, cols], func=ACT.Silu, bias=shift[b][:, t : t + 1], scale=1.0
+                )
+
+        def regroup(b, half):
+            if half == 0:
+                a_grp[b] = work.tile([P, TOKENS, PACK], BF16, name="a_grp", align_bytes=64)
+            cols = slice(half * HALF, (half + 1) * HALF)
+            nc.gpsimd.tensor_scalar(
+                out=a_grp[b][:, cols, :],
+                in0=a_pl[b][:, :, cols].rearrange("p t w -> p w t"),
+                scalar1=1.0,
+                scalar2=0.0,
+                op0=ALU.mult,
+                op1=ALU.add,
+            )
+
+        def quantise(b, half):
+            if half == 0:
+                a_codes[b] = work.tile([P, TOKENS], U32, name="a_codes", align_bytes=64)
+                a_scales[b] = work.tile([P, TOKENS], U8, name="a_scales", align_bytes=64)
+            cols = slice(half * HALF, (half + 1) * HALF)
+            nc.vector.quantize_mx(
+                out=a_codes[b][:, cols].bitcast(FP8X4),
+                scales=a_scales[b][:, cols],
+                in_=a_grp[b][:, cols, :].rearrange("p w t -> p (w t)"),
+            )
+
+        def multiply(b, j, acc, w_cols):
+            tokens = slice(j * P, (j + 1) * P)
+            nc.tensor.matmul_mx(
+                out=acc,
+                lhsT=a_codes[b][:, tokens].bitcast(FP8X4),
+                lhsT_scale=a_scales[b][:, tokens],
+                rhs=w_codes[:, w_cols].bitcast(FP8X4),
+                rhs_scale=w_scales[:, w_cols],
+                start=True,
+                stop=True,
+            )
+
+        def fill(b, k):
+            half, i = divmod(k, BANKS_PER_HALF)
+            prod[b, k] = psum.tile([P, WIDE], F32, name="prod", bufs=AHEAD)
+            if i == 0:
+                for n in range(HALF_TILES):
+                    multiply(b, half * HALF_TILES + n, prod[b, k][:, n * NARROW : (n + 1) * NARROW], slice(WIDE, D_OUT))
+            else:
+                multiply(b, half * HALF_TILES + i - 1, prod[b, k][:], slice(0, WIDE))
+
+        def drain(b, k):
+            half, i = divmod(k, BANKS_PER_HALF)
+            if i == 0:
+                tiles = slice(half * HALF_TILES, (half + 1) * HALF_TILES)
+                nc.vector.tensor_tensor(
+                    out=out_sb[b][:, tiles, WIDE:D_OUT],
+                    in0=prod[b, k][:].rearrange("p (n c) -> p n c", c=NARROW),
+                    in1=bias_bc[:, WIDE:D_OUT].unsqueeze(1).to_broadcast([P, HALF_TILES, NARROW]),
+                    op=ALU.add,
+                )
+            else:
+                j = half * HALF_TILES + i - 1
+                nc.vector.tensor_tensor(out=out_sb[b][:, j, 0:WIDE], in0=prod[b, k][:], in1=bias_bc[:, 0:WIDE], op=ALU.add)
+                if j % STORE_TILES == STORE_TILES - 1:
+                    done = slice(j + 1 - STORE_TILES, j + 1)
+                    nc.sync.dma_start(
+                        out=out[b, :, :].rearrange("(p j) c -> p j c", j=TILES)[:, done, :], in_=out_sb[b][:, done, :]
+                    )
+
+        def finish(b):
+            out_sb[b] = work.tile([P, TILES, D_OUT], F32, name="out_sb")
+            for k in range(FILLS):
+                drain(b, k)
+                if k + AHEAD < FILLS:
+                    fill(b, k + AHEAD)
+
+        def statistics(b, pair):
+            for t in range(pair * PAIR, (pair + 1) * PAIR):
+                transpose_plane(b, t)
+                centred_squares(b, t)
+            scale_of(b, pair)
+
+        token_sums(0)
+        gb_ps = psum.tile([P, P], BF16, name="gb_ps", tag="prod", bufs=AHEAD)
+        nc.tensor.transpose(gb_ps[:], gb_rows[:], ident[:])
+        gamma = const.tile([P, PACK], F32)
+        nc.vector.tensor_copy(out=gamma[:], in_=gb_ps[:, 0:PACK])
+        beta = const.tile([P, PACK], F32)
+        nc.vector.tensor_copy(out=beta[:], in_=gb_ps[:, PACK : 2 * PACK])
+
+        for pair in range(2):
+            statistics(0, pair)
+
+        pos_t = const.tile([P, PACK, TOKENS], BF16)
+        for t in range(PACK):
+            pos_ps = psum.tile([P, TOKENS], BF16, name="pos_ps", tag="prod", bufs=AHEAD)
+            for j in range(TILES):
+                nc.tensor.transpose(pos_ps[:, j * P : (j + 1) * P], pos_nat[:, j, t * P : (t + 1) * P], ident[:])
+            nc.vector.tensor_copy(out=pos_t[:, t, :], in_=pos_ps[:])
+        token_sums(1)
+
+        w_grp = const.tile([P, D_OUT, PACK], BF16, align_bytes=64)
+        w_codes = const.tile([P, D_OUT], U32, align_bytes=64)
+        w_scales = const.tile([P, D_OUT], U8, align_bytes=64)
+
+        def quantise_weights():
+            nc.vector.tensor_copy(out=w_grp[:], in_=w_raw[:].rearrange("p t n -> p n t"))
+            for w_cols in (slice(0, WIDE), slice(WIDE, D_OUT)):
+                nc.vector.quantize_mx(
+                    out=w_codes[:, w_cols].bitcast(FP8X4),
+                    scales=w_scales[:, w_cols],
+                    in_=w_grp[:, w_cols, :].rearrange("p n t -> p (n t)"),
+                )
+
+        for b in range(BATCH + 1):
+            for pair in range(2):
+                for t in range(pair * PAIR, (pair + 1) * PAIR):
+                    if b < BATCH:
+                        normalise_plane(b, t)
+                    if b + 1 < BATCH:
+                        transpose_plane(b + 1, t)
+                        centred_squares(b + 1, t)
+                if b + 1 < BATCH:
+                    scale_of(b + 1, pair)
+                if b == 1 and pair == 0:
+                    quantise_weights()
+                if b >= 1:
+                    quantise(b - 1, pair)
+                    if pair == 0:
+                        for k in range(AHEAD):
+                            fill(b - 1, k)
+            if b < BATCH:
+                shift_of(b)
+                for half in range(2):
+                    swish(b, half)
+            if b >= 1:
+                finish(b - 1)
+            if b < BATCH:
+                for half in range(2):
+                    regroup(b, half)
+            if b + 2 < BATCH:
+                token_sums(b + 2)

@@ -113,22 +113,22 @@ def tile_attentionblock_pa_t_kernel(tc, x, pos_enc, gamma1, beta1, W_qkv, b_qkv,
 
         def scale_of(b, pair):
             planes = slice(pair * PAIR, (pair + 1) * PAIR)
-            nc.scalar.activation(
-                out=var_eps[b][:, planes], in_=sum_sq[b][:, planes], func=ACT.Copy, scale=1.0 / TOKENS, bias=EPS
+            nc.gpsimd.tensor_scalar(
+                out=var_eps[b][:, planes],
+                in0=sum_sq[b][:, planes],
+                scalar1=1.0 / TOKENS,
+                scalar2=EPS,
+                op0=ALU.mult,
+                op1=ALU.add,
             )
             rstd = small.tile([P, PAIR], F32, name="rstd")
             nc.gpsimd.tensor_tensor(out=rstd[:], in0=var_eps[b][:, planes], in1=minus_half[:], op=ALU.pow)
             nc.gpsimd.tensor_tensor(out=scale[b][:, planes], in0=rstd[:], in1=gamma[:, planes], op=ALU.mult)
 
         def shift_of(b):
-            for t in range(PACK):
-                nc.scalar.activation(
-                    out=shift[b][:, t : t + 1],
-                    in_=neg_mean[b][:, t : t + 1],
-                    func=ACT.Identity,
-                    scale=scale[b][:, t : t + 1],
-                    bias=beta[:, t : t + 1],
-                )
+            moved = small.tile([P, PACK], F32, name="moved")
+            nc.gpsimd.tensor_tensor(out=moved[:], in0=neg_mean[b][:], in1=scale[b][:], op=ALU.mult)
+            nc.gpsimd.tensor_tensor(out=shift[b][:], in0=moved[:], in1=beta[:], op=ALU.add)
 
         def normalise_plane(b, t):
             if t == 0:
@@ -142,13 +142,11 @@ def tile_attentionblock_pa_t_kernel(tc, x, pos_enc, gamma1, beta1, W_qkv, b_qkv,
                 op1=ALU.add,
             )
 
-        def swish(b, half):
-            if half == 0:
-                a_pl[b] = work.tile([P, PACK, TOKENS], BF16, name="a_pl")
-            cols = slice(half * HALF, (half + 1) * HALF)
+        def swish(b):
+            a_pl[b] = work.tile([P, PACK, TOKENS], BF16, name="a_pl")
             for t in range(PACK):
                 nc.scalar.activation(
-                    out=a_pl[b][:, t, cols], in_=h_pl[b][:, t, cols], func=ACT.Silu, bias=shift[b][:, t : t + 1], scale=1.0
+                    out=a_pl[b][:, t, :], in_=h_pl[b][:, t, :], func=ACT.Silu, bias=shift[b][:, t : t + 1], scale=1.0
                 )
 
         def regroup(b, half):
@@ -215,9 +213,10 @@ def tile_attentionblock_pa_t_kernel(tc, x, pos_enc, gamma1, beta1, W_qkv, b_qkv,
                         out=out[b, :, :].rearrange("(p j) c -> p j c", j=TILES)[:, done, :], in_=out_sb[b][:, done, :]
                     )
 
-        def finish(b):
-            out_sb[b] = work.tile([P, TILES, D_OUT], F32, name="out_sb")
-            for k in range(FILLS):
+        def finish(b, half):
+            if half == 0:
+                out_sb[b] = work.tile([P, TILES, D_OUT], F32, name="out_sb")
+            for k in range(half * BANKS_PER_HALF, (half + 1) * BANKS_PER_HALF):
                 drain(b, k)
                 if k + AHEAD < FILLS:
                     fill(b, k + AHEAD)
@@ -238,6 +237,7 @@ def tile_attentionblock_pa_t_kernel(tc, x, pos_enc, gamma1, beta1, W_qkv, b_qkv,
 
         for pair in range(2):
             statistics(0, pair)
+        shift_of(0)
 
         pos_t = const.tile([P, PACK, TOKENS], BF16)
         for t in range(PACK):
@@ -260,7 +260,7 @@ def tile_attentionblock_pa_t_kernel(tc, x, pos_enc, gamma1, beta1, W_qkv, b_qkv,
                     in_=w_grp[:, w_cols, :].rearrange("p n t -> p (n t)"),
                 )
 
-        for b in range(BATCH + 1):
+        for b in range(BATCH + 2):
             for pair in range(2):
                 for t in range(pair * PAIR, (pair + 1) * PAIR):
                     if b < BATCH:
@@ -270,19 +270,22 @@ def tile_attentionblock_pa_t_kernel(tc, x, pos_enc, gamma1, beta1, W_qkv, b_qkv,
                         centred_squares(b + 1, t)
                 if b + 1 < BATCH:
                     scale_of(b + 1, pair)
-                if b == 1 and pair == 0:
-                    quantise_weights()
-                if b >= 1:
-                    quantise(b - 1, pair)
-                    if pair == 0:
-                        for k in range(AHEAD):
-                            fill(b - 1, k)
+            if b + 1 < BATCH:
+                shift_of(b + 1)
             if b < BATCH:
-                shift_of(b)
+                swish(b)
+            if b >= 2:
+                finish(b - 2, 0)
+            if b == 1:
+                quantise_weights()
+            if 1 <= b <= BATCH:
                 for half in range(2):
-                    swish(b, half)
-            if b >= 1:
-                finish(b - 1)
+                    quantise(b - 1, half)
+            if b >= 2:
+                finish(b - 2, 1)
+            if 1 <= b <= BATCH:
+                for k in range(AHEAD):
+                    fill(b - 1, k)
             if b < BATCH:
                 for half in range(2):
                     regroup(b, half)

@@ -192,7 +192,8 @@ def tile_attentionblock_pa_t_kernel(tc, x, pos_enc, gamma1, beta1, W_qkv, b_qkv,
                 for n in range(HALF_TILES):
                     multiply(b, half * HALF_TILES + n, prod[b, k][:, n * NARROW : (n + 1) * NARROW], slice(WIDE, D_OUT))
             else:
-                multiply(b, half * HALF_TILES + i - 1, prod[b, k][:], slice(0, WIDE))
+                for repeat in range(2):
+                    multiply(b, half * HALF_TILES + i - 1, prod[b, k][:], slice(0, WIDE))
 
         def drain(b, k):
             half, i = divmod(k, BANKS_PER_HALF)

@@ -73,27 +73,29 @@ def tile_attentionblock_pa_t_kernel(tc, x, pos_enc, gamma1, beta1, W_qkv, b_qkv,
         nc.vector.memset(warm[:], 0.0)
         nc.scalar.activation(out=warm[:], in_=warm[:], func=ACT.Silu)
 
-        neg_mean, sum_sq, var_eps, scale, shift = {}, {}, {}, {}, {}
+        sums, neg_mean, sum_sq, var_eps, scale, shift = {}, {}, {}, {}, {}, {}
         x_t, h_pl, a_pl, a_grp, a_codes, a_scales = {}, {}, {}, {}, {}, {}
         prod, out_sb = {}, {}
 
-        def token_sums(b):
-            sums = psum.tile([P, PACK], F32, name="sums")
-            for t in range(PACK):
+        def token_sums(b, pair):
+            if pair == 0:
+                sums[b] = psum.tile([P, PACK], F32, name="sums")
+                neg_mean[b] = small.tile([P, PACK], F32, name="neg_mean")
+                sum_sq[b] = small.tile([P, PACK], F32, name="sum_sq")
+                var_eps[b] = small.tile([P, PACK], F32, name="var_eps")
+                scale[b] = small.tile([P, PACK], F32, name="scale")
+                shift[b] = small.tile([P, PACK], F32, name="shift")
+            planes = slice(pair * PAIR, (pair + 1) * PAIR)
+            for t in range(pair * PAIR, (pair + 1) * PAIR):
                 for j in range(TILES):
                     nc.tensor.matmul(
-                        out=sums[:, t : t + 1],
+                        out=sums[b][:, t : t + 1],
                         lhsT=x_nat[b][:, j, t * P : (t + 1) * P],
                         rhs=ones[:],
                         start=(j == 0),
                         stop=(j == TILES - 1),
                     )
-            neg_mean[b] = small.tile([P, PACK], F32, name="neg_mean")
-            nc.scalar.activation(out=neg_mean[b][:], in_=sums[:], func=ACT.Copy, scale=-1.0 / TOKENS)
-            sum_sq[b] = small.tile([P, PACK], F32, name="sum_sq")
-            var_eps[b] = small.tile([P, PACK], F32, name="var_eps")
-            scale[b] = small.tile([P, PACK], F32, name="scale")
-            shift[b] = small.tile([P, PACK], F32, name="shift")
+            nc.scalar.activation(out=neg_mean[b][:, planes], in_=sums[b][:, planes], func=ACT.Copy, scale=-1.0 / TOKENS)
 
         def transpose_plane(b, t):
             x_t[b, t] = psum.tile([P, TOKENS], BF16, name="x_t", tag="x_t%d" % t)
@@ -162,15 +164,11 @@ def tile_attentionblock_pa_t_kernel(tc, x, pos_enc, gamma1, beta1, W_qkv, b_qkv,
                 op1=ALU.add,
             )
 
-        def quantise(b, half):
-            if half == 0:
-                a_codes[b] = work.tile([P, TOKENS], U32, name="a_codes", align_bytes=64)
-                a_scales[b] = work.tile([P, TOKENS], U8, name="a_scales", align_bytes=64)
-            cols = slice(half * HALF, (half + 1) * HALF)
+        def quantise(b):
+            a_codes[b] = work.tile([P, TOKENS], U32, name="a_codes", align_bytes=64)
+            a_scales[b] = work.tile([P, TOKENS], U8, name="a_scales", align_bytes=64)
             nc.vector.quantize_mx(
-                out=a_codes[b][:, cols].bitcast(FP8X4),
-                scales=a_scales[b][:, cols],
-                in_=a_grp[b][:, cols, :].rearrange("p w t -> p (w t)"),
+                out=a_codes[b][:].bitcast(FP8X4), scales=a_scales[b][:], in_=a_grp[b][:].rearrange("p w t -> p (w t)")
             )
 
         def multiply(b, j, acc, w_cols):
@@ -192,8 +190,7 @@ def tile_attentionblock_pa_t_kernel(tc, x, pos_enc, gamma1, beta1, W_qkv, b_qkv,
                 for n in range(HALF_TILES):
                     multiply(b, half * HALF_TILES + n, prod[b, k][:, n * NARROW : (n + 1) * NARROW], slice(WIDE, D_OUT))
             else:
-                for repeat in range(2):
-                    multiply(b, half * HALF_TILES + i - 1, prod[b, k][:], slice(0, WIDE))
+                multiply(b, half * HALF_TILES + i - 1, prod[b, k][:], slice(0, WIDE))
 
         def drain(b, k):
             half, i = divmod(k, BANKS_PER_HALF)
@@ -214,39 +211,35 @@ def tile_attentionblock_pa_t_kernel(tc, x, pos_enc, gamma1, beta1, W_qkv, b_qkv,
                         out=out[b, :, :].rearrange("(p j) c -> p j c", j=TILES)[:, done, :], in_=out_sb[b][:, done, :]
                     )
 
-        def finish(b, half):
-            if half == 0:
-                out_sb[b] = work.tile([P, TILES, D_OUT], F32, name="out_sb")
-            for k in range(half * BANKS_PER_HALF, (half + 1) * BANKS_PER_HALF):
+        def finish(b):
+            out_sb[b] = work.tile([P, TILES, D_OUT], F32, name="out_sb")
+            for k in range(FILLS):
                 drain(b, k)
                 if k + AHEAD < FILLS:
                     fill(b, k + AHEAD)
 
-        def statistics(b, pair):
-            for t in range(pair * PAIR, (pair + 1) * PAIR):
-                transpose_plane(b, t)
-                centred_squares(b, t)
-            scale_of(b, pair)
-
-        token_sums(0)
-        gb_ps = psum.tile([P, P], BF16, name="gb_ps", tag="prod", bufs=AHEAD)
-        nc.tensor.transpose(gb_ps[:], gb_rows[:], ident[:])
         gamma = const.tile([P, PACK], F32)
-        nc.vector.tensor_copy(out=gamma[:], in_=gb_ps[:, 0:PACK])
         beta = const.tile([P, PACK], F32)
-        nc.vector.tensor_copy(out=beta[:], in_=gb_ps[:, PACK : 2 * PACK])
-
-        for pair in range(2):
-            statistics(0, pair)
-        shift_of(0)
-
         pos_t = const.tile([P, PACK, TOKENS], BF16)
-        for t in range(PACK):
-            pos_ps = psum.tile([P, TOKENS], BF16, name="pos_ps", tag="prod", bufs=AHEAD)
-            for j in range(TILES):
-                nc.tensor.transpose(pos_ps[:, j * P : (j + 1) * P], pos_nat[:, j, t * P : (t + 1) * P], ident[:])
-            nc.vector.tensor_copy(out=pos_t[:, t, :], in_=pos_ps[:])
-        token_sums(1)
+        for pair in range(2):
+            token_sums(0, pair)
+            if pair == 0:
+                gb_ps = psum.tile([P, P], BF16, name="gb_ps", tag="prod", bufs=AHEAD)
+                nc.tensor.transpose(gb_ps[:], gb_rows[:], ident[:])
+                nc.vector.tensor_copy(out=gamma[:], in_=gb_ps[:, 0:PACK])
+                nc.vector.tensor_copy(out=beta[:], in_=gb_ps[:, PACK : 2 * PACK])
+            for t in range(pair * PAIR, (pair + 1) * PAIR):
+                transpose_plane(0, t)
+                centred_squares(0, t)
+            scale_of(0, pair)
+            for t in range(pair * PAIR, (pair + 1) * PAIR):
+                pos_ps = psum.tile([P, TOKENS], BF16, name="pos_ps", tag="prod", bufs=AHEAD)
+                for j in range(TILES):
+                    nc.tensor.transpose(pos_ps[:, j * P : (j + 1) * P], pos_nat[:, j, t * P : (t + 1) * P], ident[:])
+                nc.scalar.copy(out=pos_t[:, t, :], in_=pos_ps[:])
+        shift_of(0)
+        for pair in range(2):
+            token_sums(1, pair)
 
         w_grp = const.tile([P, D_OUT, PACK], BF16, align_bytes=64)
         w_codes = const.tile([P, D_OUT], U32, align_bytes=64)
@@ -276,19 +269,16 @@ def tile_attentionblock_pa_t_kernel(tc, x, pos_enc, gamma1, beta1, W_qkv, b_qkv,
             if b < BATCH:
                 swish(b)
             if b >= 2:
-                finish(b - 2, 0)
+                finish(b - 2)
             if b == 1:
                 quantise_weights()
             if 1 <= b <= BATCH:
-                for half in range(2):
-                    quantise(b - 1, half)
-            if b >= 2:
-                finish(b - 2, 1)
-            if 1 <= b <= BATCH:
+                quantise(b - 1)
                 for k in range(AHEAD):
                     fill(b - 1, k)
             if b < BATCH:
                 for half in range(2):
                     regroup(b, half)
             if b + 2 < BATCH:
-                token_sums(b + 2)
+                for pair in range(2):
+                    token_sums(b + 2, pair)

from contextlib import ExitStack

import concourse.masks as masks
import concourse.mybir as mybir

F32 = mybir.dt.float32
BF16 = mybir.dt.bfloat16
U32 = mybir.dt.uint32
U8 = mybir.dt.uint8
FP8X4 = mybir.dt.float8_e4m3fn_x4
ACT = mybir.ActivationFunctionType
ALU = mybir.AluOpType

P = 128
PACK = 4
BATCH = 8
TOKENS = 1024
D_IN = P * PACK
D_OUT = 640
TILES = TOKENS // P
HALF_TILES = TILES // 2
HALF = TOKENS // 2
PAIR = PACK // 2
WIDE = 512
NARROW = D_OUT - WIDE
BANKS_PER_HALF = 1 + HALF_TILES
FILLS = 2 * BANKS_PER_HALF
AHEAD = 3
STORE_TILES = 2
EPS = 1e-5

FLOPS = 2 * BATCH * TOKENS * D_IN * D_OUT


def tile_attentionblock_pa_t_kernel(tc, x, pos_enc, gamma1, beta1, W_qkv, b_qkv, out):
    nc = tc.nc
    with ExitStack() as ctx:
        const = ctx.enter_context(tc.tile_pool(name="const", bufs=1))
        work = ctx.enter_context(tc.tile_pool(name="work", bufs=2))
        small = ctx.enter_context(tc.tile_pool(name="small", bufs=4))
        psum = ctx.enter_context(tc.psum_pool(name="psum", bufs=1))
        ctx.enter_context(tc.manual_schedule())

        gb_rows = const.tile([P, P], BF16)
        nc.vector.memset(gb_rows[:], 0.0)

        x_nat = {}

        def load_x(b):
            x_nat[b] = const.tile([P, TILES, D_IN], BF16, name="x%d" % b)
            nc.sync.dma_start(out=x_nat[b][:], in_=x[b, :, :].rearrange("(p j) d -> p j d", j=TILES))

        load_x(0)
        nc.sync.dma_start(out=gb_rows[0:PACK, :], in_=gamma1[0, :, :].rearrange("a (t p) -> (a t) p", p=P))
        nc.sync.dma_start(out=gb_rows[PACK : 2 * PACK, :], in_=beta1[0, :, :].rearrange("a (t p) -> (a t) p", p=P))
        pos_nat = const.tile([P, TILES, D_IN], BF16)
        nc.sync.dma_start(out=pos_nat[:], in_=pos_enc[0, :, :].rearrange("(p j) d -> p j d", j=TILES))
        load_x(1)
        w_raw = const.tile([P, PACK, D_OUT], BF16)
        nc.sync.dma_start(out=w_raw[:], in_=W_qkv.rearrange("(t p) n -> p t n", p=P))
        bias_bc = const.tile([P, D_OUT], BF16)
        nc.sync.dma_start(out=bias_bc[:], in_=b_qkv.partition_broadcast(P))
        for b in range(2, BATCH):
            load_x(b)

        ident = const.tile([P, P], BF16)
        masks.make_identity(nc, ident[:])
        ones = const.tile([P, 1], BF16)
        nc.vector.memset(ones[:], 1.0)
        minus_half = const.tile([P, PAIR], F32)
        nc.vector.memset(minus_half[:], -0.5)
        warm = const.tile([P, 1], F32)
        nc.vector.memset(warm[:], 0.0)
        nc.scalar.activation(out=warm[:], in_=warm[:], func=ACT.Silu)

        sums, neg_mean, sum_sq, var_eps, scale, shift = {}, {}, {}, {}, {}, {}
        x_t, h_pl, a_pl, a_grp, a_codes, a_scales = {}, {}, {}, {}, {}, {}
        prod, out_sb = {}, {}

        def token_sums(b, pair):
            if pair == 0:
                sums[b] = psum.tile([P, PACK], F32, name="sums")
                neg_mean[b] = small.tile([P, PACK], F32, name="neg_mean")
                sum_sq[b] = small.tile([P, PACK], F32, name="sum_sq")
                var_eps[b] = small.tile([P, PACK], F32, name="var_eps")
                scale[b] = small.tile([P, PACK], F32, name="scale")
                shift[b] = small.tile([P, PACK], F32, name="shift")
            planes = slice(pair * PAIR, (pair + 1) * PAIR)
            for t in range(pair * PAIR, (pair + 1) * PAIR):
                for j in range(TILES):
                    nc.tensor.matmul(
                        out=sums[b][:, t : t + 1],
                        lhsT=x_nat[b][:, j, t * P : (t + 1) * P],
                        rhs=ones[:],
                        start=(j == 0),
                        stop=(j == TILES - 1),
                    )
            nc.scalar.activation(out=neg_mean[b][:, planes], in_=sums[b][:, planes], func=ACT.Copy, scale=-1.0 / TOKENS)

        def transpose_plane(b, t):
            x_t[b, t] = psum.tile([P, TOKENS], BF16, name="x_t", tag="x_t%d" % t)
            for j in range(TILES):
                nc.tensor.transpose(x_t[b, t][:, j * P : (j + 1) * P], x_nat[b][:, j, t * P : (t + 1) * P], ident[:])

        def centred_squares(b, t):
            unused = work.tile([P, TOKENS], BF16, name="unused")
            nc.scalar.activation(
                out=unused[:],
                in_=x_t[b, t][:],
                func=ACT.Square,
                bias=neg_mean[b][:, t : t + 1],
                scale=1.0,
                accum_out=sum_sq[b][:, t : t + 1],
            )

        def scale_of(b, pair):
            planes = slice(pair * PAIR, (pair + 1) * PAIR)
            nc.gpsimd.tensor_scalar(
                out=var_eps[b][:, planes],
                in0=sum_sq[b][:, planes],
                scalar1=1.0 / TOKENS,
                scalar2=EPS,
                op0=ALU.mult,
                op1=ALU.add,
            )
            rstd = small.tile([P, PAIR], F32, name="rstd")
            nc.gpsimd.tensor_tensor(out=rstd[:], in0=var_eps[b][:, planes], in1=minus_half[:], op=ALU.pow)
            nc.gpsimd.tensor_tensor(out=scale[b][:, planes], in0=rstd[:], in1=gamma[:, planes], op=ALU.mult)

        def shift_of(b):
            moved = small.tile([P, PACK], F32, name="moved")
            nc.gpsimd.tensor_tensor(out=moved[:], in0=neg_mean[b][:], in1=scale[b][:], op=ALU.mult)
            nc.gpsimd.tensor_tensor(out=shift[b][:], in0=moved[:], in1=beta[:], op=ALU.add)

        def normalise_plane(b, t):
            if t == 0:
                h_pl[b] = work.tile([P, PACK, TOKENS], F32, name="h_pl")
            nc.vector.scalar_tensor_tensor(
                out=h_pl[b][:, t, :],
                in0=x_t[b, t][:],
                scalar=scale[b][:, t : t + 1],
                in1=pos_t[:, t, :],
                op0=ALU.mult,
                op1=ALU.add,
            )

        def swish(b):
            a_pl[b] = work.tile([P, PACK, TOKENS], BF16, name="a_pl")
            for t in range(PACK):
                nc.scalar.activation(
                    out=a_pl[b][:, t, :], in_=h_pl[b][:, t, :], func=ACT.Silu, bias=shift[b][:, t : t + 1], scale=1.0
                )

        def regroup(b, half):
            if half == 0:
                a_grp[b] = work.tile([P, TOKENS, PACK], BF16, name="a_grp", align_bytes=64)
            cols = slice(half * HALF, (half + 1) * HALF)
            nc.gpsimd.tensor_scalar(
                out=a_grp[b][:, cols, :],
                in0=a_pl[b][:, :, cols].rearrange("p t w -> p w t"),
                scalar1=1.0,
                scalar2=0.0,
                op0=ALU.mult,
                op1=ALU.add,
            )

        def quantise(b):
            a_codes[b] = work.tile([P, TOKENS], U32, name="a_codes", align_bytes=64)
            a_scales[b] = work.tile([P, TOKENS], U8, name="a_scales", align_bytes=64)
            nc.vector.quantize_mx(
                out=a_codes[b][:].bitcast(FP8X4), scales=a_scales[b][:], in_=a_grp[b][:].rearrange("p w t -> p (w t)")
            )

        def multiply(b, j, acc, w_cols):
            tokens = slice(j * P, (j + 1) * P)
            nc.tensor.matmul_mx(
                out=acc,
                lhsT=a_codes[b][:, tokens].bitcast(FP8X4),
                lhsT_scale=a_scales[b][:, tokens],
                rhs=w_codes[:, w_cols].bitcast(FP8X4),
                rhs_scale=w_scales[:, w_cols],
                start=True,
                stop=True,
            )

        def fill(b, k):
            half, i = divmod(k, BANKS_PER_HALF)
            prod[b, k] = psum.tile([P, WIDE], F32, name="prod", bufs=AHEAD)
            if i == 0:
                for n in range(HALF_TILES):
                    multiply(b, half * HALF_TILES + n, prod[b, k][:, n * NARROW : (n + 1) * NARROW], slice(WIDE, D_OUT))
            else:
                multiply(b, half * HALF_TILES + i - 1, prod[b, k][:], slice(0, WIDE))

        def drain(b, k):
            half, i = divmod(k, BANKS_PER_HALF)
            if i == 0:
                tiles = slice(half * HALF_TILES, (half + 1) * HALF_TILES)
                nc.vector.tensor_tensor(
                    out=out_sb[b][:, tiles, WIDE:D_OUT],
                    in0=prod[b, k][:].rearrange("p (n c) -> p n c", c=NARROW),
                    in1=bias_bc[:, WIDE:D_OUT].unsqueeze(1).to_broadcast([P, HALF_TILES, NARROW]),
                    op=ALU.add,
                )
            else:
                j = half * HALF_TILES + i - 1
                nc.vector.tensor_tensor(out=out_sb[b][:, j, 0:WIDE], in0=prod[b, k][:], in1=bias_bc[:, 0:WIDE], op=ALU.add)
                if j % STORE_TILES == STORE_TILES - 1:
                    done = slice(j + 1 - STORE_TILES, j + 1)
                    nc.sync.dma_start(
                        out=out[b, :, :].rearrange("(p j) c -> p j c", j=TILES)[:, done, :], in_=out_sb[b][:, done, :]
                    )

        def finish(b):
            out_sb[b] = work.tile([P, TILES, D_OUT], F32, name="out_sb")
            for k in range(FILLS):
                drain(b, k)
                if k + AHEAD < FILLS:
                    fill(b, k + AHEAD)

        gamma = const.tile([P, PACK], F32)
        beta = const.tile([P, PACK], F32)
        pos_t = const.tile([P, PACK, TOKENS], BF16)
        for pair in range(2):
            token_sums(0, pair)
            if pair == 0:
                gb_ps = psum.tile([P, P], BF16, name="gb_ps", tag="prod", bufs=AHEAD)
                nc.tensor.transpose(gb_ps[:], gb_rows[:], ident[:])
                nc.vector.tensor_copy(out=gamma[:], in_=gb_ps[:, 0:PACK])
                nc.vector.tensor_copy(out=beta[:], in_=gb_ps[:, PACK : 2 * PACK])
            for t in range(pair * PAIR, (pair + 1) * PAIR):
                transpose_plane(0, t)
                centred_squares(0, t)
            scale_of(0, pair)
            for t in range(pair * PAIR, (pair + 1) * PAIR):
                pos_ps = psum.tile([P, TOKENS], BF16, name="pos_ps", tag="prod", bufs=AHEAD)
                for j in range(TILES):
                    nc.tensor.transpose(pos_ps[:, j * P : (j + 1) * P], pos_nat[:, j, t * P : (t + 1) * P], ident[:])
                nc.scalar.copy(out=pos_t[:, t, :], in_=pos_ps[:])
        shift_of(0)
        for pair in range(2):
            token_sums(1, pair)

        w_grp = const.tile([P, D_OUT, PACK], BF16, align_bytes=64)
        w_codes = const.tile([P, D_OUT], U32, align_bytes=64)
        w_scales = const.tile([P, D_OUT], U8, align_bytes=64)

        def quantise_weights():
            nc.vector.tensor_copy(out=w_grp[:], in_=w_raw[:].rearrange("p t n -> p n t"))
            for w_cols in (slice(0, WIDE), slice(WIDE, D_OUT)):
                nc.vector.quantize_mx(
                    out=w_codes[:, w_cols].bitcast(FP8X4),
                    scales=w_scales[:, w_cols],
                    in_=w_grp[:, w_cols, :].rearrange("p n t -> p (n t)"),
                )

        for b in range(BATCH + 2):
            for pair in range(2):
                for t in range(pair * PAIR, (pair + 1) * PAIR):
                    if b < BATCH:
                        normalise_plane(b, t)
                    if b + 1 < BATCH:
                        transpose_plane(b + 1, t)
                        centred_squares(b + 1, t)
                if b + 1 < BATCH:
                    scale_of(b + 1, pair)
            if b + 1 < BATCH:
                shift_of(b + 1)
            if b < BATCH:
                swish(b)
            if b >= 2:
                finish(b - 2)
            if b == 1:
                quantise_weights()
            if 1 <= b <= BATCH:
                quantise(b - 1)
                for k in range(AHEAD):
                    fill(b - 1, k)
            if b < BATCH:
                for half in range(2):
                    regroup(b, half)
            if b + 2 < BATCH:
                for pair in range(2):
                    token_sums(b + 2, pair)
